import numpy as np
import ml_dtypes


def mxq(x, axis, fmt="e4m3"):
    dtype, down = {"e4m3": (ml_dtypes.float8_e4m3fn, 7), "e5m2": (ml_dtypes.float8_e5m2, 14)}[fmt]
    v = np.moveaxis(np.asarray(x, np.float32).astype(ml_dtypes.bfloat16).astype(np.float64), axis, -1)
    blocks = v.reshape(v.shape[:-1] + (-1, 32))
    amax = np.abs(blocks).max(-1, keepdims=True)
    byte = np.maximum(np.where(amax > 0, np.frexp(amax)[1] - 1 + 127, 0) - down, 1)
    scale = np.exp2(byte - 127.0)
    codes = (blocks / scale).astype(np.float32).astype(dtype).astype(np.float64)
    return np.moveaxis((codes * scale).reshape(v.shape), -1, axis)


WIDE = False


def mx_kscale(k):
    if not WIDE:
        return np.ones(k)
    levels = np.array([10, -10, 5, -5, 0])
    a = np.random.permutation(np.resize(levels, k // 512 * 4)).reshape(k // 512, 4)
    idx = np.arange(k)
    return np.exp2(a[idx // 512, idx % 128 // 32])


BF16 = ml_dtypes.bfloat16


def bf(x):
    return np.asarray(x, np.float32).astype(BF16)


def f64(x):
    return np.asarray(x).astype(np.float64)


E2M1 = np.array([0.0, 0.5, 1.0, 1.5, 2.0, 3.0, 4.0, 6.0, -0.0, -0.5, -1.0, -1.5, -2.0, -3.0, -4.0, -6.0])


def pack_weight(w, fmt):
    k, n = w.shape
    w = f64(bf(w)).reshape(k // 32, 32, n)
    amax = np.abs(w).max(1)
    if fmt == "e4m3":
        byte = np.frexp(amax)[1] - 1 + 127 - 7
    else:
        mant, ex = np.frexp(amax / 6.0)
        byte = np.where(mant > 0.5, ex, ex - 1) + 127
    byte = np.clip(np.where(amax > 0, byte, 1), 1, 254)
    scaled = (w * np.exp2(127.0 - byte)[:, None, :]).reshape(k, n).astype(np.float32)
    by_word = np.ascontiguousarray(scaled.reshape(k // 512, 128, 4, n).transpose(0, 1, 3, 2))
    if fmt == "e4m3":
        words = by_word.astype(ml_dtypes.float8_e4m3fn).view(np.uint8)
    else:
        c = by_word.astype(ml_dtypes.float4_e2m1fn).view(np.uint8) & 0xF
        words = c[..., 0::2] | (c[..., 1::2] << 4)
    return np.ascontiguousarray(words), np.ascontiguousarray(byte.astype(np.uint8).reshape(k // 512, 16, n))


def unpack_weight(words, scales, fmt):
    g, p, n, _ = words.shape
    if fmt == "e4m3":
        vals = np.ascontiguousarray(words).view(ml_dtypes.float8_e4m3fn).astype(np.float64)
    else:
        nib = np.empty((g, p, n, 4), np.uint8)
        nib[..., 0::2] = words & 0xF
        nib[..., 1::2] = words >> 4
        vals = E2M1[nib]
    vals = vals * np.repeat(np.exp2(scales.astype(np.float64) - 127.0), 8, axis=1)[..., None]
    return vals.transpose(0, 1, 3, 2).reshape(g * 512, n)

def pack4(w):
    words, scales = pack_weight(w, "e2m1")
    return words.reshape(words.shape[0], 128, -1), scales


def unpack4(words, scales):
    return unpack_weight(words.reshape(words.shape[0], 128, -1, 2), scales, "e2m1")


N, C, F, G = 4096, 3, 128, 512
F2 = F + F
F3 = F2 + F


def silu(v):
    return v / (1.0 + np.exp(-v))


def setup_inputs():
    s = mx_kscale(G)
    h = bf(silu(1.4 * np.random.standard_normal((N, 1, G))) * s)
    mu_W = bf(np.random.standard_normal((N, C, F)))
    mu_VW = bf(np.sqrt(C) * np.random.standard_normal((N, 1, F)))
    q = bf(np.random.standard_normal((N, 1, F)))
    mu = bf(np.random.standard_normal((N, C, F)))
    W2 = np.random.standard_normal((F3, G)) / np.sqrt(G) / s
    words, scales = pack4(np.ascontiguousarray(W2.T))
    b2 = bf(0.2 * np.random.standard_normal(F3))
    return {"h": h,
            "mu_W": mu_W,
            "mu_VW": mu_VW,
            "q": q,
            "mu": mu,
            "W2_words": words,
            "W2_scales": scales,
            "b2": b2}


def reference(h, mu_W, mu_VW, q, mu, W2_words, W2_scales, b2):
    x = (mxq(f64(h), 2, "e4m3") @ unpack4(W2_words, W2_scales)) + f64(b2)
    dq_intra = x[..., :F]
    dmu_intra = x[..., F:F2] * f64(mu_W)
    dqmu_intra = x[..., F2:] * f64(mu_VW)
    q_out = f64(q) + dq_intra + dqmu_intra
    mu_out = f64(mu) + dmu_intra
    return q_out, mu_out

@@ -1,0 +1,219 @@
+from contextlib import ExitStack
+
+import concourse.mybir as mybir
+from concourse.masks import make_identity
+
+F32 = mybir.dt.float32
+BF16 = mybir.dt.bfloat16
+U8 = mybir.dt.uint8
+U32 = mybir.dt.uint32
+I32 = mybir.dt.int32
+FP8X4 = mybir.dt.float8_e4m3fn_x4
+FP4X4 = mybir.dt.float4_e2m1fn_x4
+ADD = mybir.AluOpType.add
+MULT = mybir.AluOpType.mult
+IDENTITY = mybir.ActivationFunctionType.Identity
+
+P = 128
+N_ATOMS = 4096
+C = 3
+F = 128
+K = 512
+PACK = 4
+N_BLOCKS = 3
+DQ, DMU, DQMU = 0, 1, 2
+BLOCK_ORDER = (DMU, DQMU, DQ)
+
+ATOMS_PER_PARTITION = N_ATOMS // P
+TILES_PER_GROUP = 4
+GROUP_ATOMS = TILES_PER_GROUP * P
+N_GROUPS = ATOMS_PER_PARTITION // TILES_PER_GROUP
+WORDS = K // 2
+TILES_PER_BANK = 2
+Q_PARTS = 2
+GROUPS_PER_PART = N_GROUPS // Q_PARTS
+ATOMS_PER_PART = ATOMS_PER_PARTITION // Q_PARTS
+
+FLOPS = 2 * N_ATOMS * K * N_BLOCKS * F
+
+
+def tile_painnmixing_pb_t_kernel(
+    tc, h, mu_W, mu_VW, q, mu, W2_words, W2_scales, b2, out_0, out_1
+):
+    nc = tc.nc
+
+    h_rows = h.rearrange("(p j) o k -> p j (o k)", j=ATOMS_PER_PARTITION)
+    mu_w_rows = mu_W.rearrange("(p j) c f -> p j (c f)", j=ATOMS_PER_PARTITION)
+    mu_rows = mu.rearrange("(p j) c f -> p j (c f)", j=ATOMS_PER_PARTITION)
+    mu_vw_rows = mu_VW.rearrange("(p j) o f -> p j (o f)", j=ATOMS_PER_PARTITION)
+    q_rows = q.rearrange("(p j) o f -> p j (o f)", j=ATOMS_PER_PARTITION)
+    q_out_rows = out_0.rearrange("(p j) o f -> p j (o f)", j=ATOMS_PER_PARTITION)
+    mu_out_rows = out_1.rearrange("(p j) c f -> p j (c f)", j=ATOMS_PER_PARTITION)
+
+    with ExitStack() as ctx:
+        ctx.enter_context(tc.manual_schedule())
+        consts = ctx.enter_context(tc.tile_pool(name="consts", bufs=1))
+        loads = ctx.enter_context(tc.tile_pool(name="loads", bufs=N_GROUPS))
+        parts = ctx.enter_context(tc.tile_pool(name="parts", bufs=Q_PARTS))
+        outs = ctx.enter_context(tc.tile_pool(name="outs", bufs=N_GROUPS))
+        stage = ctx.enter_context(tc.tile_pool(name="stage", bufs=2))
+        biased = ctx.enter_context(tc.tile_pool(name="biased", bufs=2 * N_BLOCKS))
+        psum_h = ctx.enter_context(tc.psum_pool(name="psum_h", bufs=2))
+        psum_x = ctx.enter_context(tc.psum_pool(name="psum_x", bufs=N_BLOCKS))
+        psum_b = ctx.enter_context(tc.psum_pool(name="psum_b", bufs=N_BLOCKS))
+
+        h_sb, mu_w_sb, mu_sb, mu_vw_sb, q_sb = {}, {}, {}, {}, {}
+        grouped_of, codes_of, scales_of, x_t_of, x_of = {}, {}, {}, {}, {}
+
+        def group_atoms(g):
+            return slice(TILES_PER_GROUP * g, TILES_PER_GROUP * (g + 1))
+
+        def load_h(g):
+            h_sb[g] = loads.tile([P, TILES_PER_GROUP, K], BF16, name="h_sb")
+            nc.sync.dma_start(out=h_sb[g][:], in_=h_rows[:, group_atoms(g), :])
+
+        ident = consts.tile([P, P], F32, name="ident")
+        make_identity(nc, ident[:])
+
+        w_scales = consts.tile([P, N_BLOCKS * F], U8, name="w_scales", align_bytes=64)
+        nc.vector.memset(w_scales[:].bitcast(I32), 0)
+        bias_rows = consts.tile([P, F], BF16, name="bias_rows")
+        nc.vector.memset(bias_rows[:], 0.0)
+        nc.scalar.dma_start(
+            out=bias_rows[0:N_BLOCKS, :], in_=b2.rearrange("(b f) -> b f", f=F)
+        )
+
+        load_h(0)
+        w_words = consts.tile([P, 2 * N_BLOCKS * F], U8, name="w_words", align_bytes=64)
+        nc.sync.dma_start(out=w_words[:].bitcast(I32), in_=W2_words[0].bitcast(I32))
+        for quad in range(4):
+            nc.sync.dma_start(
+                out=w_scales[32 * quad : 32 * quad + 4, :].bitcast(I32),
+                in_=W2_scales[0, 4 * quad : 4 * quad + 4, :].bitcast(I32),
+            )
+        for g in range(N_GROUPS):
+            if g + 1 < N_GROUPS:
+                load_h(g + 1)
+            if g % GROUPS_PER_PART == 0:
+                part = g // GROUPS_PER_PART
+                part_atoms = slice(ATOMS_PER_PART * part, ATOMS_PER_PART * (part + 1))
+                mu_vw_sb[part] = parts.tile([P, ATOMS_PER_PART, F], BF16, name="mu_vw_sb")
+                nc.sync.dma_start(out=mu_vw_sb[part][:], in_=mu_vw_rows[:, part_atoms, :])
+                q_sb[part] = parts.tile([P, ATOMS_PER_PART, F], BF16, name="q_sb")
+                nc.sync.dma_start(out=q_sb[part][:], in_=q_rows[:, part_atoms, :])
+            mu_w_sb[g] = loads.tile([P, TILES_PER_GROUP, C * F], BF16, name="mu_w_sb")
+            nc.sync.dma_start(out=mu_w_sb[g][:], in_=mu_w_rows[:, group_atoms(g), :])
+            mu_sb[g] = loads.tile([P, TILES_PER_GROUP, C * F], BF16, name="mu_sb")
+            nc.sync.dma_start(out=mu_sb[g][:], in_=mu_rows[:, group_atoms(g), :])
+
+        bias_rows_f32 = consts.tile([P, F], F32, name="bias_rows_f32")
+        nc.vector.tensor_copy(out=bias_rows_f32[:], in_=bias_rows[:])
+        bias_bank = psum_b.tile([P, TILES_PER_GROUP, F], F32, name="x_bank")
+        nc.tensor.transpose(out=bias_bank[:, 0, :], in_=bias_rows_f32[:], identity=ident[:])
+        bias_col = consts.tile([P, N_BLOCKS], F32, name="bias_col")
+        nc.scalar.activation(out=bias_col[:], in_=bias_bank[:, 0, 0:N_BLOCKS], func=IDENTITY)
+
+        def transpose_h(g):
+            words = h_sb[g][:].rearrange("p j k -> p (j k)").bitcast(F32)
+            grouped_of[g] = stage.tile(
+                [P, TILES_PER_GROUP, P, PACK], BF16, name="grouped", align_bytes=64
+            )
+            grouped_words = (
+                grouped_of[g][:]
+                .rearrange("p j a t -> p (j a t)")
+                .bitcast(F32)
+                .rearrange("p (j a u) -> p j a u", j=TILES_PER_GROUP, u=2)
+            )
+            for first in range(0, TILES_PER_GROUP, TILES_PER_BANK):
+                h_t = psum_h.tile([P, TILES_PER_BANK, 2, P], F32, name="h_t")
+                for local in range(TILES_PER_BANK):
+                    start = WORDS * (first + local)
+                    for u in range(2):
+                        nc.tensor.transpose(
+                            out=h_t[:, local, u, :],
+                            in_=words[:, start + u : start + WORDS : 2],
+                            identity=ident[:],
+                        )
+                nc.scalar.copy(
+                    out=grouped_words[:, first : first + TILES_PER_BANK, :, :],
+                    in_=h_t[:].rearrange("p j u a -> p j a u"),
+                )
+
+        def quantise(g):
+            codes_of[g] = stage.tile([P, GROUP_ATOMS], U32, name="codes", align_bytes=64)
+            scales_of[g] = stage.tile([P, GROUP_ATOMS], U8, name="scales", align_bytes=64)
+            nc.vector.quantize_mx(
+                out=codes_of[g][:].bitcast(FP8X4),
+                scales=scales_of[g][:],
+                in_=grouped_of[g][:].rearrange("p j a t -> p (j a t)"),
+            )
+
+        def multiply(g):
+            x_t_of[g] = {}
+            for b in BLOCK_ORDER:
+                acc = psum_x.tile([P, GROUP_ATOMS], F32, name="acc")
+                nc.tensor.matmul_mx(
+                    out=acc[:],
+                    lhsT=w_words[:, 2 * F * b : 2 * F * (b + 1)].bitcast(FP4X4),
+                    lhsT_scale=w_scales[:, F * b : F * (b + 1)],
+                    rhs=codes_of[g][:].bitcast(FP8X4),
+                    rhs_scale=scales_of[g][:],
+                    start=True,
+                    stop=True,
+                )
+                x_t_of[g][b] = biased.tile([P, GROUP_ATOMS], F32, name="x_t")
+                nc.scalar.activation(
+                    out=x_t_of[g][b][:],
+                    in_=acc[:],
+                    func=IDENTITY,
+                    bias=bias_col[:, b : b + 1],
+                    scale=1.0,
+                )
+
+        def turn_back(g):
+            x_of[g] = {}
+            for b in BLOCK_ORDER:
+                x_of[g][b] = psum_b.tile([P, TILES_PER_GROUP, F], F32, name="x_bank")
+                for j in range(TILES_PER_GROUP):
+                    nc.tensor.transpose(
+                        out=x_of[g][b][:, j, :],
+                        in_=x_t_of[g][b][:, P * j : P * (j + 1)],
+                        identity=ident[:],
+                    )
+
+        def gate_and_store(g):
+            part = g // GROUPS_PER_PART
+            first = TILES_PER_GROUP * (g % GROUPS_PER_PART)
+            in_part = slice(first, first + TILES_PER_GROUP)
+            mu_new = outs.tile([P, TILES_PER_GROUP, C, F], F32, name="mu_new")
+            nc.vector.tensor_tensor(
+                out=mu_new[:],
+                in0=x_of[g][DMU][:].unsqueeze(2).to_broadcast([P, TILES_PER_GROUP, C, F]),
+                in1=mu_w_sb[g][:].rearrange("p j (c f) -> p j c f", c=C),
+                op=MULT,
+            )
+            mu_flat = mu_new[:].rearrange("p j c f -> p j (c f)")
+            nc.gpsimd.tensor_tensor(out=mu_flat, in0=mu_flat, in1=mu_sb[g][:], op=ADD)
+            q_gated = stage.tile([P, TILES_PER_GROUP, F], F32, name="q_gated")
+            nc.vector.tensor_tensor(
+                out=q_gated[:], in0=x_of[g][DQMU][:], in1=mu_vw_sb[part][:, in_part, :], op=MULT
+            )
+            q_new = outs.tile([P, TILES_PER_GROUP, F], F32, name="q_new")
+            nc.vector.tensor_tensor(
+                out=q_new[:], in0=x_of[g][DQ][:], in1=q_sb[part][:, in_part, :], op=ADD
+            )
+            nc.vector.tensor_tensor(out=q_new[:], in0=q_new[:], in1=q_gated[:], op=ADD)
+            nc.sync.dma_start(out=q_out_rows[:, group_atoms(g), :], in_=q_new[:])
+            nc.sync.dma_start(out=mu_out_rows[:, group_atoms(g), :], in_=mu_flat)
+
+        for s in range(N_GROUPS + 2):
+            if s >= 2:
+                turn_back(s - 2)
+            if s < N_GROUPS:
+                transpose_h(s)
+            if 1 <= s <= N_GROUPS:
+                multiply(s - 1)
+            if s >= 2:
+                gate_and_store(s - 2)
+            if s < N_GROUPS:
+                quantise(s)

@@ -193,7 +193,7 @@ def tile_painnmixing_pb_t_kernel(
                 op=MULT,
             )
             mu_flat = mu_new[:].rearrange("p j c f -> p j (c f)")
-            nc.gpsimd.tensor_tensor(out=mu_flat, in0=mu_flat, in1=mu_sb[g][:], op=ADD)
+            nc.vector.tensor_tensor(out=mu_flat, in0=mu_flat, in1=mu_sb[g][:], op=ADD)
             q_gated = stage.tile([P, TILES_PER_GROUP, F], F32, name="q_gated")
             nc.vector.tensor_tensor(
                 out=q_gated[:], in0=x_of[g][DQMU][:], in1=mu_vw_sb[part][:, in_part, :], op=MULT

@@ -22,7 +22,7 @@ K = 512
 PACK = 4
 N_BLOCKS = 3
 DQ, DMU, DQMU = 0, 1, 2
-BLOCK_ORDER = (DMU, DQMU, DQ)
+BLOCK_ORDER = (DQMU, DQ, DMU)
 
 ATOMS_PER_PARTITION = N_ATOMS // P
 TILES_PER_GROUP = 4
@@ -185,15 +185,6 @@ def tile_painnmixing_pb_t_kernel(
             part = g // GROUPS_PER_PART
             first = TILES_PER_GROUP * (g % GROUPS_PER_PART)
             in_part = slice(first, first + TILES_PER_GROUP)
-            mu_new = outs.tile([P, TILES_PER_GROUP, C, F], F32, name="mu_new")
-            nc.vector.tensor_tensor(
-                out=mu_new[:],
-                in0=x_of[g][DMU][:].unsqueeze(2).to_broadcast([P, TILES_PER_GROUP, C, F]),
-                in1=mu_w_sb[g][:].rearrange("p j (c f) -> p j c f", c=C),
-                op=MULT,
-            )
-            mu_flat = mu_new[:].rearrange("p j c f -> p j (c f)")
-            nc.vector.tensor_tensor(out=mu_flat, in0=mu_flat, in1=mu_sb[g][:], op=ADD)
             q_gated = stage.tile([P, TILES_PER_GROUP, F], F32, name="q_gated")
             nc.vector.tensor_tensor(
                 out=q_gated[:], in0=x_of[g][DQMU][:], in1=mu_vw_sb[part][:, in_part, :], op=MULT
@@ -202,7 +193,16 @@ def tile_painnmixing_pb_t_kernel(
             nc.vector.tensor_tensor(
                 out=q_new[:], in0=x_of[g][DQ][:], in1=q_sb[part][:, in_part, :], op=ADD
             )
+            mu_new = outs.tile([P, TILES_PER_GROUP, C, F], F32, name="mu_new")
+            nc.vector.tensor_tensor(
+                out=mu_new[:],
+                in0=x_of[g][DMU][:].unsqueeze(2).to_broadcast([P, TILES_PER_GROUP, C, F]),
+                in1=mu_w_sb[g][:].rearrange("p j (c f) -> p j c f", c=C),
+                op=MULT,
+            )
             nc.vector.tensor_tensor(out=q_new[:], in0=q_new[:], in1=q_gated[:], op=ADD)
+            mu_flat = mu_new[:].rearrange("p j c f -> p j (c f)")
+            nc.gpsimd.tensor_tensor(out=mu_flat, in0=mu_flat, in1=mu_sb[g][:], op=ADD)
             nc.sync.dma_start(out=q_out_rows[:, group_atoms(g), :], in_=q_new[:])
             nc.sync.dma_start(out=mu_out_rows[:, group_atoms(g), :], in_=mu_flat)
 

@@ -30,6 +30,7 @@ GROUP_ATOMS = TILES_PER_GROUP * P
 N_GROUPS = ATOMS_PER_PARTITION // TILES_PER_GROUP
 WORDS = K // 2
 TILES_PER_BANK = 2
+H_AHEAD = 2
 Q_PARTS = 2
 GROUPS_PER_PART = N_GROUPS // Q_PARTS
 ATOMS_PER_PART = ATOMS_PER_PARTITION // Q_PARTS
@@ -57,6 +58,7 @@ def tile_painnmixing_pb_t_kernel(
         parts = ctx.enter_context(tc.tile_pool(name="parts", bufs=Q_PARTS))
         outs = ctx.enter_context(tc.tile_pool(name="outs", bufs=N_GROUPS))
         stage = ctx.enter_context(tc.tile_pool(name="stage", bufs=2))
+        regroup = ctx.enter_context(tc.tile_pool(name="regroup", bufs=3))
         biased = ctx.enter_context(tc.tile_pool(name="biased", bufs=2 * N_BLOCKS))
         psum_h = ctx.enter_context(tc.psum_pool(name="psum_h", bufs=2))
         psum_x = ctx.enter_context(tc.psum_pool(name="psum_x", bufs=N_BLOCKS))
@@ -64,6 +66,7 @@ def tile_painnmixing_pb_t_kernel(
 
         h_sb, mu_w_sb, mu_sb, mu_vw_sb, q_sb = {}, {}, {}, {}, {}
         grouped_of, codes_of, scales_of, x_t_of, x_of = {}, {}, {}, {}, {}
+        mu_new_of = {}
 
         def group_atoms(g):
             return slice(TILES_PER_GROUP * g, TILES_PER_GROUP * (g + 1))
@@ -91,9 +94,11 @@ def tile_painnmixing_pb_t_kernel(
                 out=w_scales[32 * quad : 32 * quad + 4, :].bitcast(I32),
                 in_=W2_scales[0, 4 * quad : 4 * quad + 4, :].bitcast(I32),
             )
+        for g in range(1, H_AHEAD + 1):
+            load_h(g)
         for g in range(N_GROUPS):
-            if g + 1 < N_GROUPS:
-                load_h(g + 1)
+            if g + H_AHEAD + 1 < N_GROUPS:
+                load_h(g + H_AHEAD + 1)
             if g % GROUPS_PER_PART == 0:
                 part = g // GROUPS_PER_PART
                 part_atoms = slice(ATOMS_PER_PART * part, ATOMS_PER_PART * (part + 1))
@@ -112,10 +117,12 @@ def tile_painnmixing_pb_t_kernel(
         nc.tensor.transpose(out=bias_bank[:, 0, :], in_=bias_rows_f32[:], identity=ident[:])
         bias_col = consts.tile([P, N_BLOCKS], F32, name="bias_col")
         nc.scalar.activation(out=bias_col[:], in_=bias_bank[:, 0, 0:N_BLOCKS], func=IDENTITY)
+        ident_bf16 = consts.tile([P, P], BF16, name="ident_bf16")
+        nc.vector.tensor_copy(out=ident_bf16[:], in_=ident[:])
 
         def transpose_h(g):
             words = h_sb[g][:].rearrange("p j k -> p (j k)").bitcast(F32)
-            grouped_of[g] = stage.tile(
+            grouped_of[g] = regroup.tile(
                 [P, TILES_PER_GROUP, P, PACK], BF16, name="grouped", align_bytes=64
             )
             grouped_words = (
@@ -170,50 +177,85 @@ def tile_painnmixing_pb_t_kernel(
                     scale=1.0,
                 )
 
+        def part_atoms_of(g):
+            first = TILES_PER_GROUP * (g % GROUPS_PER_PART)
+            return slice(first, first + TILES_PER_GROUP)
+
         def turn_back(g):
             x_of[g] = {}
             for b in BLOCK_ORDER:
                 x_of[g][b] = psum_b.tile([P, TILES_PER_GROUP, F], F32, name="x_bank")
+                if b == DQ:
+                    nc.tensor.matmul(
+                        out=x_of[g][b][:].rearrange("p j f -> p (j f)"),
+                        lhsT=ident_bf16[:],
+                        rhs=q_sb[g // GROUPS_PER_PART][:, part_atoms_of(g), :].rearrange(
+                            "p j f -> p (j f)"
+                        ),
+                        start=True,
+                        stop=False,
+                    )
                 for j in range(TILES_PER_GROUP):
-                    nc.tensor.transpose(
+                    nc.tensor.matmul(
                         out=x_of[g][b][:, j, :],
-                        in_=x_t_of[g][b][:, P * j : P * (j + 1)],
-                        identity=ident[:],
+                        lhsT=x_t_of[g][b][:, P * j : P * (j + 1)],
+                        rhs=ident[:],
+                        is_transpose=True,
+                        start=(b != DQ),
+                        stop=(b != DQ or j == TILES_PER_GROUP - 1),
                     )
 
-        def gate_and_store(g):
-            part = g // GROUPS_PER_PART
-            first = TILES_PER_GROUP * (g % GROUPS_PER_PART)
-            in_part = slice(first, first + TILES_PER_GROUP)
+        def update_q(g):
             q_gated = stage.tile([P, TILES_PER_GROUP, F], F32, name="q_gated")
             nc.vector.tensor_tensor(
-                out=q_gated[:], in0=x_of[g][DQMU][:], in1=mu_vw_sb[part][:, in_part, :], op=MULT
+                out=q_gated[:],
+                in0=x_of[g][DQMU][:],
+                in1=mu_vw_sb[g // GROUPS_PER_PART][:, part_atoms_of(g), :],
+                op=MULT,
             )
             q_new = outs.tile([P, TILES_PER_GROUP, F], F32, name="q_new")
+            nc.vector.tensor_tensor(out=q_new[:], in0=x_of[g][DQ][:], in1=q_gated[:], op=ADD)
+            nc.sync.dma_start(out=q_out_rows[:, group_atoms(g), :], in_=q_new[:])
+
+        def gate_mu(g):
+            mu_new_of[g] = outs.tile([P, TILES_PER_GROUP, C * F], F32, name="mu_new")
             nc.vector.tensor_tensor(
-                out=q_new[:], in0=x_of[g][DQ][:], in1=q_sb[part][:, in_part, :], op=ADD
-            )
-            mu_new = outs.tile([P, TILES_PER_GROUP, C, F], F32, name="mu_new")
-            nc.vector.tensor_tensor(
-                out=mu_new[:],
+                out=mu_new_of[g][:].rearrange("p j (c f) -> p j c f", c=C),
                 in0=x_of[g][DMU][:].unsqueeze(2).to_broadcast([P, TILES_PER_GROUP, C, F]),
                 in1=mu_w_sb[g][:].rearrange("p j (c f) -> p j c f", c=C),
                 op=MULT,
             )
-            nc.vector.tensor_tensor(out=q_new[:], in0=q_new[:], in1=q_gated[:], op=ADD)
-            mu_flat = mu_new[:].rearrange("p j c f -> p j (c f)")
-            nc.gpsimd.tensor_tensor(out=mu_flat, in0=mu_flat, in1=mu_sb[g][:], op=ADD)
-            nc.sync.dma_start(out=q_out_rows[:, group_atoms(g), :], in_=q_new[:])
-            nc.sync.dma_start(out=mu_out_rows[:, group_atoms(g), :], in_=mu_flat)
 
+        def add_mu_and_store(engine, g, first, count):
+            tiles = slice(first, first + count)
+            atoms = slice(TILES_PER_GROUP * g + first, TILES_PER_GROUP * g + first + count)
+            engine.tensor_tensor(
+                out=mu_new_of[g][:, tiles, :],
+                in0=mu_new_of[g][:, tiles, :],
+                in1=mu_sb[g][:, tiles, :],
+                op=ADD,
+            )
+            nc.sync.dma_start(out=mu_out_rows[:, atoms, :], in_=mu_new_of[g][:, tiles, :])
+
+        def update_mu(g):
+            if g < N_GROUPS - 1:
+                add_mu_and_store(nc.gpsimd, g, 0, TILES_PER_GROUP)
+            else:
+                for first in range(0, TILES_PER_GROUP, TILES_PER_GROUP // 2):
+                    add_mu_and_store(nc.vector, g, first, TILES_PER_GROUP // 2)
+
+        transpose_h(0)
         for s in range(N_GROUPS + 2):
             if s >= 2:
                 turn_back(s - 2)
-            if s < N_GROUPS:
-                transpose_h(s)
             if 1 <= s <= N_GROUPS:
                 multiply(s - 1)
+            if s + 1 < N_GROUPS:
+                transpose_h(s + 1)
             if s >= 2:
-                gate_and_store(s - 2)
+                update_q(s - 2)
+                gate_mu(s - 2)
             if s < N_GROUPS:
                 quantise(s)
+            if s >= 2:
+                update_mu(s - 2)

@@ -31,9 +31,9 @@ N_GROUPS = ATOMS_PER_PARTITION // TILES_PER_GROUP
 WORDS = K // 2
 TILES_PER_BANK = 2
 H_AHEAD = 2
-Q_PARTS = 2
-GROUPS_PER_PART = N_GROUPS // Q_PARTS
-ATOMS_PER_PART = ATOMS_PER_PARTITION // Q_PARTS
+MU_GROUPS = 2
+Q_GROUPS = 4
+Q_OUT_GROUPS = 2
 
 FLOPS = 2 * N_ATOMS * K * N_BLOCKS * F
 
@@ -55,8 +55,10 @@ def tile_painnmixing_pb_t_kernel(
         ctx.enter_context(tc.manual_schedule())
         consts = ctx.enter_context(tc.tile_pool(name="consts", bufs=1))
         loads = ctx.enter_context(tc.tile_pool(name="loads", bufs=N_GROUPS))
-        parts = ctx.enter_context(tc.tile_pool(name="parts", bufs=Q_PARTS))
+        mu_loads = ctx.enter_context(tc.tile_pool(name="mu_loads", bufs=N_GROUPS // MU_GROUPS))
+        q_loads = ctx.enter_context(tc.tile_pool(name="q_loads", bufs=N_GROUPS // Q_GROUPS))
         outs = ctx.enter_context(tc.tile_pool(name="outs", bufs=N_GROUPS))
+        q_outs = ctx.enter_context(tc.tile_pool(name="q_outs", bufs=N_GROUPS // Q_OUT_GROUPS))
         stage = ctx.enter_context(tc.tile_pool(name="stage", bufs=2))
         regroup = ctx.enter_context(tc.tile_pool(name="regroup", bufs=3))
         biased = ctx.enter_context(tc.tile_pool(name="biased", bufs=2 * N_BLOCKS))
@@ -66,14 +68,23 @@ def tile_painnmixing_pb_t_kernel(
 
         h_sb, mu_w_sb, mu_sb, mu_vw_sb, q_sb = {}, {}, {}, {}, {}
         grouped_of, codes_of, scales_of, x_t_of, x_of = {}, {}, {}, {}, {}
-        mu_new_of = {}
+        mu_new_of, q_new = {}, {}
 
-        def group_atoms(g):
-            return slice(TILES_PER_GROUP * g, TILES_PER_GROUP * (g + 1))
+        def atoms_of(first_group, groups):
+            return slice(TILES_PER_GROUP * first_group, TILES_PER_GROUP * (first_group + groups))
 
         def load_h(g):
             h_sb[g] = loads.tile([P, TILES_PER_GROUP, K], BF16, name="h_sb")
-            nc.sync.dma_start(out=h_sb[g][:], in_=h_rows[:, group_atoms(g), :])
+            nc.sync.dma_start(out=h_sb[g][:], in_=h_rows[:, atoms_of(g, 1), :])
+
+        def load_groups(pool, tiles, rows, g, groups, name):
+            tiles[g // groups] = pool.tile(
+                [P, TILES_PER_GROUP * groups, rows.shape[2]], BF16, name=name
+            )
+            nc.sync.dma_start(out=tiles[g // groups][:], in_=rows[:, atoms_of(g, groups), :])
+
+        def group_of(tiles, g, groups):
+            return tiles[g // groups][:, atoms_of(g % groups, 1), :]
 
         ident = consts.tile([P, P], F32, name="ident")
         make_identity(nc, ident[:])
@@ -99,17 +110,12 @@ def tile_painnmixing_pb_t_kernel(
         for g in range(N_GROUPS):
             if g + H_AHEAD + 1 < N_GROUPS:
                 load_h(g + H_AHEAD + 1)
-            if g % GROUPS_PER_PART == 0:
-                part = g // GROUPS_PER_PART
-                part_atoms = slice(ATOMS_PER_PART * part, ATOMS_PER_PART * (part + 1))
-                mu_vw_sb[part] = parts.tile([P, ATOMS_PER_PART, F], BF16, name="mu_vw_sb")
-                nc.sync.dma_start(out=mu_vw_sb[part][:], in_=mu_vw_rows[:, part_atoms, :])
-                q_sb[part] = parts.tile([P, ATOMS_PER_PART, F], BF16, name="q_sb")
-                nc.sync.dma_start(out=q_sb[part][:], in_=q_rows[:, part_atoms, :])
-            mu_w_sb[g] = loads.tile([P, TILES_PER_GROUP, C * F], BF16, name="mu_w_sb")
-            nc.sync.dma_start(out=mu_w_sb[g][:], in_=mu_w_rows[:, group_atoms(g), :])
-            mu_sb[g] = loads.tile([P, TILES_PER_GROUP, C * F], BF16, name="mu_sb")
-            nc.sync.dma_start(out=mu_sb[g][:], in_=mu_rows[:, group_atoms(g), :])
+            if g % Q_GROUPS == 0:
+                load_groups(q_loads, mu_vw_sb, mu_vw_rows, g, Q_GROUPS, "mu_vw_sb")
+                load_groups(q_loads, q_sb, q_rows, g, Q_GROUPS, "q_sb")
+            if g % MU_GROUPS == 0:
+                load_groups(mu_loads, mu_w_sb, mu_w_rows, g, MU_GROUPS, "mu_w_sb")
+                load_groups(mu_loads, mu_sb, mu_rows, g, MU_GROUPS, "mu_sb")
 
         bias_rows_f32 = consts.tile([P, F], F32, name="bias_rows_f32")
         nc.vector.tensor_copy(out=bias_rows_f32[:], in_=bias_rows[:])
@@ -177,10 +183,6 @@ def tile_painnmixing_pb_t_kernel(
                     scale=1.0,
                 )
 
-        def part_atoms_of(g):
-            first = TILES_PER_GROUP * (g % GROUPS_PER_PART)
-            return slice(first, first + TILES_PER_GROUP)
-
         def turn_back(g):
             x_of[g] = {}
             for b in BLOCK_ORDER:
@@ -189,9 +191,7 @@ def tile_painnmixing_pb_t_kernel(
                     nc.tensor.matmul(
                         out=x_of[g][b][:].rearrange("p j f -> p (j f)"),
                         lhsT=ident_bf16[:],
-                        rhs=q_sb[g // GROUPS_PER_PART][:, part_atoms_of(g), :].rearrange(
-                            "p j f -> p (j f)"
-                        ),
+                        rhs=group_of(q_sb, g, Q_GROUPS).rearrange("p j f -> p (j f)"),
                         start=True,
                         stop=False,
                     )
@@ -210,19 +210,28 @@ def tile_painnmixing_pb_t_kernel(
             nc.vector.tensor_tensor(
                 out=q_gated[:],
                 in0=x_of[g][DQMU][:],
-                in1=mu_vw_sb[g // GROUPS_PER_PART][:, part_atoms_of(g), :],
+                in1=group_of(mu_vw_sb, g, Q_GROUPS),
                 op=MULT,
             )
-            q_new = outs.tile([P, TILES_PER_GROUP, F], F32, name="q_new")
-            nc.vector.tensor_tensor(out=q_new[:], in0=x_of[g][DQ][:], in1=q_gated[:], op=ADD)
-            nc.sync.dma_start(out=q_out_rows[:, group_atoms(g), :], in_=q_new[:])
+            if g % Q_OUT_GROUPS == 0:
+                q_new[g // Q_OUT_GROUPS] = q_outs.tile(
+                    [P, TILES_PER_GROUP * Q_OUT_GROUPS, F], F32, name="q_new"
+                )
+            nc.vector.tensor_tensor(
+                out=group_of(q_new, g, Q_OUT_GROUPS), in0=x_of[g][DQ][:], in1=q_gated[:], op=ADD
+            )
+            if g % Q_OUT_GROUPS == Q_OUT_GROUPS - 1:
+                nc.sync.dma_start(
+                    out=q_out_rows[:, atoms_of(g + 1 - Q_OUT_GROUPS, Q_OUT_GROUPS), :],
+                    in_=q_new[g // Q_OUT_GROUPS][:],
+                )
 
         def gate_mu(g):
             mu_new_of[g] = outs.tile([P, TILES_PER_GROUP, C * F], F32, name="mu_new")
             nc.vector.tensor_tensor(
                 out=mu_new_of[g][:].rearrange("p j (c f) -> p j c f", c=C),
                 in0=x_of[g][DMU][:].unsqueeze(2).to_broadcast([P, TILES_PER_GROUP, C, F]),
-                in1=mu_w_sb[g][:].rearrange("p j (c f) -> p j c f", c=C),
+                in1=group_of(mu_w_sb, g, MU_GROUPS).rearrange("p j (c f) -> p j c f", c=C),
                 op=MULT,
             )
 
@@ -232,7 +241,7 @@ def tile_painnmixing_pb_t_kernel(
             engine.tensor_tensor(
                 out=mu_new_of[g][:, tiles, :],
                 in0=mu_new_of[g][:, tiles, :],
-                in1=mu_sb[g][:, tiles, :],
+                in1=group_of(mu_sb, g, MU_GROUPS)[:, tiles, :],
                 op=ADD,
             )
             nc.sync.dma_start(out=mu_out_rows[:, atoms, :], in_=mu_new_of[g][:, tiles, :])

@@ -22,7 +22,7 @@ K = 512
 PACK = 4
 N_BLOCKS = 3
 DQ, DMU, DQMU = 0, 1, 2
-BLOCK_ORDER = (DQMU, DQ, DMU)
+BLOCK_ORDER = (DQMU, DMU, DQ)
 
 ATOMS_PER_PARTITION = N_ATOMS // P
 TILES_PER_GROUP = 4
@@ -68,7 +68,7 @@ def tile_painnmixing_pb_t_kernel(
 
         h_sb, mu_w_sb, mu_sb, mu_vw_sb, q_sb = {}, {}, {}, {}, {}
         grouped_of, codes_of, scales_of, x_t_of, x_of = {}, {}, {}, {}, {}
-        mu_new_of, q_new = {}, {}
+        mu_new_of, q_new, q_gated_of = {}, {}, {}
 
         def atoms_of(first_group, groups):
             return slice(TILES_PER_GROUP * first_group, TILES_PER_GROUP * (first_group + groups))
@@ -112,9 +112,11 @@ def tile_painnmixing_pb_t_kernel(
                 load_h(g + H_AHEAD + 1)
             if g % Q_GROUPS == 0:
                 load_groups(q_loads, mu_vw_sb, mu_vw_rows, g, Q_GROUPS, "mu_vw_sb")
-                load_groups(q_loads, q_sb, q_rows, g, Q_GROUPS, "q_sb")
             if g % MU_GROUPS == 0:
                 load_groups(mu_loads, mu_w_sb, mu_w_rows, g, MU_GROUPS, "mu_w_sb")
+            if g % Q_GROUPS == 0:
+                load_groups(q_loads, q_sb, q_rows, g, Q_GROUPS, "q_sb")
+            if g % MU_GROUPS == 0:
                 load_groups(mu_loads, mu_sb, mu_rows, g, MU_GROUPS, "mu_sb")
 
         bias_rows_f32 = consts.tile([P, F], F32, name="bias_rows_f32")
@@ -205,20 +207,25 @@ def tile_painnmixing_pb_t_kernel(
                         stop=(b != DQ or j == TILES_PER_GROUP - 1),
                     )
 
-        def update_q(g):
-            q_gated = stage.tile([P, TILES_PER_GROUP, F], F32, name="q_gated")
+        def gate_q(g):
+            q_gated_of[g] = stage.tile([P, TILES_PER_GROUP, F], F32, name="q_gated")
             nc.vector.tensor_tensor(
-                out=q_gated[:],
+                out=q_gated_of[g][:],
                 in0=x_of[g][DQMU][:],
                 in1=group_of(mu_vw_sb, g, Q_GROUPS),
                 op=MULT,
             )
+
+        def sum_q(g):
             if g % Q_OUT_GROUPS == 0:
                 q_new[g // Q_OUT_GROUPS] = q_outs.tile(
                     [P, TILES_PER_GROUP * Q_OUT_GROUPS, F], F32, name="q_new"
                 )
             nc.vector.tensor_tensor(
-                out=group_of(q_new, g, Q_OUT_GROUPS), in0=x_of[g][DQ][:], in1=q_gated[:], op=ADD
+                out=group_of(q_new, g, Q_OUT_GROUPS),
+                in0=x_of[g][DQ][:],
+                in1=q_gated_of[g][:],
+                op=ADD,
             )
             if g % Q_OUT_GROUPS == Q_OUT_GROUPS - 1:
                 nc.sync.dma_start(
@@ -262,9 +269,10 @@ def tile_painnmixing_pb_t_kernel(
             if s + 1 < N_GROUPS:
                 transpose_h(s + 1)
             if s >= 2:
-                update_q(s - 2)
+                gate_q(s - 2)
                 gate_mu(s - 2)
             if s < N_GROUPS:
                 quantise(s)
             if s >= 2:
+                sum_q(s - 2)
                 update_mu(s - 2)

@@ -93,7 +93,7 @@ def tile_painnmixing_pb_t_kernel(
         nc.vector.memset(w_scales[:].bitcast(I32), 0)
         bias_rows = consts.tile([P, F], BF16, name="bias_rows")
         nc.vector.memset(bias_rows[:], 0.0)
-        nc.scalar.dma_start(
+        nc.gpsimd.dma_start(
             out=bias_rows[0:N_BLOCKS, :], in_=b2.rearrange("(b f) -> b f", f=F)
         )
 
@@ -119,14 +119,16 @@ def tile_painnmixing_pb_t_kernel(
             if g % MU_GROUPS == 0:
                 load_groups(mu_loads, mu_sb, mu_rows, g, MU_GROUPS, "mu_sb")
 
-        bias_rows_f32 = consts.tile([P, F], F32, name="bias_rows_f32")
-        nc.vector.tensor_copy(out=bias_rows_f32[:], in_=bias_rows[:])
-        bias_bank = psum_b.tile([P, TILES_PER_GROUP, F], F32, name="x_bank")
-        nc.tensor.transpose(out=bias_bank[:, 0, :], in_=bias_rows_f32[:], identity=ident[:])
-        bias_col = consts.tile([P, N_BLOCKS], F32, name="bias_col")
-        nc.scalar.activation(out=bias_col[:], in_=bias_bank[:, 0, 0:N_BLOCKS], func=IDENTITY)
         ident_bf16 = consts.tile([P, P], BF16, name="ident_bf16")
         nc.vector.tensor_copy(out=ident_bf16[:], in_=ident[:])
+        bias_rows_f32 = consts.tile([P, F], F32, name="bias_rows_f32")
+        bias_col = consts.tile([P, N_BLOCKS], F32, name="bias_col")
+
+        def bias_to_partitions():
+            nc.vector.tensor_copy(out=bias_rows_f32[:], in_=bias_rows[:])
+            bias_bank = psum_b.tile([P, TILES_PER_GROUP, F], F32, name="x_bank")
+            nc.tensor.transpose(out=bias_bank[:, 0, :], in_=bias_rows_f32[:], identity=ident[:])
+            nc.scalar.activation(out=bias_col[:], in_=bias_bank[:, 0, 0:N_BLOCKS], func=IDENTITY)
 
         def transpose_h(g):
             words = h_sb[g][:].rearrange("p j k -> p (j k)").bitcast(F32)
@@ -261,6 +263,7 @@ def tile_painnmixing_pb_t_kernel(
                     add_mu_and_store(nc.vector, g, first, TILES_PER_GROUP // 2)
 
         transpose_h(0)
+        bias_to_partitions()
         for s in range(N_GROUPS + 2):
             if s >= 2:
                 turn_back(s - 2)

@@ -34,6 +34,7 @@ H_AHEAD = 2
 MU_GROUPS = 2
 Q_GROUPS = 4
 Q_OUT_GROUPS = 2
+DMA_ALIGN = 256
 
 FLOPS = 2 * N_ATOMS * K * N_BLOCKS * F
 
@@ -74,12 +75,12 @@ def tile_painnmixing_pb_t_kernel(
             return slice(TILES_PER_GROUP * first_group, TILES_PER_GROUP * (first_group + groups))
 
         def load_h(g):
-            h_sb[g] = loads.tile([P, TILES_PER_GROUP, K], BF16, name="h_sb")
+            h_sb[g] = loads.tile([P, TILES_PER_GROUP, K], BF16, name="h_sb", align_bytes=DMA_ALIGN)
             nc.sync.dma_start(out=h_sb[g][:], in_=h_rows[:, atoms_of(g, 1), :])
 
         def load_groups(pool, tiles, rows, g, groups, name):
             tiles[g // groups] = pool.tile(
-                [P, TILES_PER_GROUP * groups, rows.shape[2]], BF16, name=name
+                [P, TILES_PER_GROUP * groups, rows.shape[2]], BF16, name=name, align_bytes=DMA_ALIGN
             )
             nc.sync.dma_start(out=tiles[g // groups][:], in_=rows[:, atoms_of(g, groups), :])
 
@@ -221,7 +222,7 @@ def tile_painnmixing_pb_t_kernel(
         def sum_q(g):
             if g % Q_OUT_GROUPS == 0:
                 q_new[g // Q_OUT_GROUPS] = q_outs.tile(
-                    [P, TILES_PER_GROUP * Q_OUT_GROUPS, F], F32, name="q_new"
+                    [P, TILES_PER_GROUP * Q_OUT_GROUPS, F], F32, name="q_new", align_bytes=DMA_ALIGN
                 )
             nc.vector.tensor_tensor(
                 out=group_of(q_new, g, Q_OUT_GROUPS),
@@ -236,7 +237,9 @@ def tile_painnmixing_pb_t_kernel(
                 )
 
         def gate_mu(g):
-            mu_new_of[g] = outs.tile([P, TILES_PER_GROUP, C * F], F32, name="mu_new")
+            mu_new_of[g] = outs.tile(
+                [P, TILES_PER_GROUP, C * F], F32, name="mu_new", align_bytes=DMA_ALIGN
+            )
             nc.vector.tensor_tensor(
                 out=mu_new_of[g][:].rearrange("p j (c f) -> p j c f", c=C),
                 in0=x_of[g][DMU][:].unsqueeze(2).to_broadcast([P, TILES_PER_GROUP, C, F]),

@@ -25,6 +25,7 @@ DQ, DMU, DQMU = 0, 1, 2
 BLOCK_ORDER = (DQMU, DMU, DQ)
 
 ATOMS_PER_PARTITION = N_ATOMS // P
+RUN_ATOMS = 16
 TILES_PER_GROUP = 4
 GROUP_ATOMS = TILES_PER_GROUP * P
 N_GROUPS = ATOMS_PER_PARTITION // TILES_PER_GROUP
@@ -44,13 +45,13 @@ def tile_painnmixing_pb_t_kernel(
 ):
     nc = tc.nc
 
-    h_rows = h.rearrange("(p j) o k -> p j (o k)", j=ATOMS_PER_PARTITION)
-    mu_w_rows = mu_W.rearrange("(p j) c f -> p j (c f)", j=ATOMS_PER_PARTITION)
-    mu_rows = mu.rearrange("(p j) c f -> p j (c f)", j=ATOMS_PER_PARTITION)
-    mu_vw_rows = mu_VW.rearrange("(p j) o f -> p j (o f)", j=ATOMS_PER_PARTITION)
-    q_rows = q.rearrange("(p j) o f -> p j (o f)", j=ATOMS_PER_PARTITION)
-    q_out_rows = out_0.rearrange("(p j) o f -> p j (o f)", j=ATOMS_PER_PARTITION)
-    mu_out_rows = out_1.rearrange("(p j) c f -> p j (c f)", j=ATOMS_PER_PARTITION)
+    h_rows = h.rearrange("(b p j) o k -> p b j (o k)", p=P, j=RUN_ATOMS)
+    mu_w_rows = mu_W.rearrange("(b p j) c f -> p b j (c f)", p=P, j=RUN_ATOMS)
+    mu_rows = mu.rearrange("(b p j) c f -> p b j (c f)", p=P, j=RUN_ATOMS)
+    mu_vw_rows = mu_VW.rearrange("(b p j) o f -> p b j (o f)", p=P, j=RUN_ATOMS)
+    q_rows = q.rearrange("(b p j) o f -> p b j (o f)", p=P, j=RUN_ATOMS)
+    q_out_rows = out_0.rearrange("(b p j) o f -> p b j (o f)", p=P, j=RUN_ATOMS)
+    mu_out_rows = out_1.rearrange("(b p j) c f -> p b j (c f)", p=P, j=RUN_ATOMS)
 
     with ExitStack() as ctx:
         ctx.enter_context(tc.manual_schedule())
@@ -74,15 +75,19 @@ def tile_painnmixing_pb_t_kernel(
         def atoms_of(first_group, groups):
             return slice(TILES_PER_GROUP * first_group, TILES_PER_GROUP * (first_group + groups))
 
+        def in_dram(rows, first_tile, tiles):
+            block, start = divmod(first_tile, RUN_ATOMS)
+            return rows[:, block, start : start + tiles, :]
+
         def load_h(g):
             h_sb[g] = loads.tile([P, TILES_PER_GROUP, K], BF16, name="h_sb", align_bytes=DMA_ALIGN)
-            nc.sync.dma_start(out=h_sb[g][:], in_=h_rows[:, atoms_of(g, 1), :])
+            nc.sync.dma_start(out=h_sb[g][:], in_=in_dram(h_rows, TILES_PER_GROUP * g, TILES_PER_GROUP))
 
         def load_groups(pool, tiles, rows, g, groups, name):
             tiles[g // groups] = pool.tile(
-                [P, TILES_PER_GROUP * groups, rows.shape[2]], BF16, name=name, align_bytes=DMA_ALIGN
+                [P, TILES_PER_GROUP * groups, rows.shape[3]], BF16, name=name, align_bytes=DMA_ALIGN
             )
-            nc.sync.dma_start(out=tiles[g // groups][:], in_=rows[:, atoms_of(g, groups), :])
+            nc.sync.dma_start(out=tiles[g // groups][:], in_=in_dram(rows, TILES_PER_GROUP * g, TILES_PER_GROUP * groups))
 
         def group_of(tiles, g, groups):
             return tiles[g // groups][:, atoms_of(g % groups, 1), :]
@@ -232,7 +237,7 @@ def tile_painnmixing_pb_t_kernel(
             )
             if g % Q_OUT_GROUPS == Q_OUT_GROUPS - 1:
                 nc.sync.dma_start(
-                    out=q_out_rows[:, atoms_of(g + 1 - Q_OUT_GROUPS, Q_OUT_GROUPS), :],
+                    out=in_dram(q_out_rows, TILES_PER_GROUP * (g + 1 - Q_OUT_GROUPS), TILES_PER_GROUP * Q_OUT_GROUPS),
                     in_=q_new[g // Q_OUT_GROUPS][:],
                 )
 
@@ -249,14 +254,13 @@ def tile_painnmixing_pb_t_kernel(
 
         def add_mu_and_store(engine, g, first, count):
             tiles = slice(first, first + count)
-            atoms = slice(TILES_PER_GROUP * g + first, TILES_PER_GROUP * g + first + count)
             engine.tensor_tensor(
                 out=mu_new_of[g][:, tiles, :],
                 in0=mu_new_of[g][:, tiles, :],
                 in1=group_of(mu_sb, g, MU_GROUPS)[:, tiles, :],
                 op=ADD,
             )
-            nc.sync.dma_start(out=mu_out_rows[:, atoms, :], in_=mu_new_of[g][:, tiles, :])
+            nc.sync.dma_start(out=in_dram(mu_out_rows, TILES_PER_GROUP * g + first, count), in_=mu_new_of[g][:, tiles, :])
 
         def update_mu(g):
             if g < N_GROUPS - 1:

from contextlib import ExitStack

import concourse.mybir as mybir
from concourse.masks import make_identity

F32 = mybir.dt.float32
BF16 = mybir.dt.bfloat16
U8 = mybir.dt.uint8
U32 = mybir.dt.uint32
I32 = mybir.dt.int32
FP8X4 = mybir.dt.float8_e4m3fn_x4
FP4X4 = mybir.dt.float4_e2m1fn_x4
ADD = mybir.AluOpType.add
MULT = mybir.AluOpType.mult
IDENTITY = mybir.ActivationFunctionType.Identity

P = 128
N_ATOMS = 4096
C = 3
F = 128
K = 512
PACK = 4
N_BLOCKS = 3
DQ, DMU, DQMU = 0, 1, 2
BLOCK_ORDER = (DQMU, DMU, DQ)

ATOMS_PER_PARTITION = N_ATOMS // P
RUN_ATOMS = 16
TILES_PER_GROUP = 4
GROUP_ATOMS = TILES_PER_GROUP * P
N_GROUPS = ATOMS_PER_PARTITION // TILES_PER_GROUP
WORDS = K // 2
TILES_PER_BANK = 2
H_AHEAD = 2
MU_GROUPS = 2
Q_GROUPS = 4
Q_OUT_GROUPS = 2
DMA_ALIGN = 256

FLOPS = 2 * N_ATOMS * K * N_BLOCKS * F


def tile_painnmixing_pb_t_kernel(
    tc, h, mu_W, mu_VW, q, mu, W2_words, W2_scales, b2, out_0, out_1
):
    nc = tc.nc

    h_rows = h.rearrange("(b p j) o k -> p b j (o k)", p=P, j=RUN_ATOMS)
    mu_w_rows = mu_W.rearrange("(b p j) c f -> p b j (c f)", p=P, j=RUN_ATOMS)
    mu_rows = mu.rearrange("(b p j) c f -> p b j (c f)", p=P, j=RUN_ATOMS)
    mu_vw_rows = mu_VW.rearrange("(b p j) o f -> p b j (o f)", p=P, j=RUN_ATOMS)
    q_rows = q.rearrange("(b p j) o f -> p b j (o f)", p=P, j=RUN_ATOMS)
    q_out_rows = out_0.rearrange("(b p j) o f -> p b j (o f)", p=P, j=RUN_ATOMS)
    mu_out_rows = out_1.rearrange("(b p j) c f -> p b j (c f)", p=P, j=RUN_ATOMS)

    with ExitStack() as ctx:
        ctx.enter_context(tc.manual_schedule())
        consts = ctx.enter_context(tc.tile_pool(name="consts", bufs=1))
        loads = ctx.enter_context(tc.tile_pool(name="loads", bufs=N_GROUPS))
        mu_loads = ctx.enter_context(tc.tile_pool(name="mu_loads", bufs=N_GROUPS // MU_GROUPS))
        q_loads = ctx.enter_context(tc.tile_pool(name="q_loads", bufs=N_GROUPS // Q_GROUPS))
        outs = ctx.enter_context(tc.tile_pool(name="outs", bufs=N_GROUPS))
        q_outs = ctx.enter_context(tc.tile_pool(name="q_outs", bufs=N_GROUPS // Q_OUT_GROUPS))
        stage = ctx.enter_context(tc.tile_pool(name="stage", bufs=2))
        regroup = ctx.enter_context(tc.tile_pool(name="regroup", bufs=3))
        biased = ctx.enter_context(tc.tile_pool(name="biased", bufs=2 * N_BLOCKS))
        psum_h = ctx.enter_context(tc.psum_pool(name="psum_h", bufs=2))
        psum_x = ctx.enter_context(tc.psum_pool(name="psum_x", bufs=N_BLOCKS))
        psum_b = ctx.enter_context(tc.psum_pool(name="psum_b", bufs=N_BLOCKS))

        h_sb, mu_w_sb, mu_sb, mu_vw_sb, q_sb = {}, {}, {}, {}, {}
        grouped_of, codes_of, scales_of, x_t_of, x_of = {}, {}, {}, {}, {}
        mu_new_of, q_new, q_gated_of = {}, {}, {}

        def atoms_of(first_group, groups):
            return slice(TILES_PER_GROUP * first_group, TILES_PER_GROUP * (first_group + groups))

        def in_dram(rows, first_tile, tiles):
            block, start = divmod(first_tile, RUN_ATOMS)
            return rows[:, block, start : start + tiles, :]

        def load_h(g):
            h_sb[g] = loads.tile([P, TILES_PER_GROUP, K], BF16, name="h_sb", align_bytes=DMA_ALIGN)
            nc.sync.dma_start(out=h_sb[g][:], in_=in_dram(h_rows, TILES_PER_GROUP * g, TILES_PER_GROUP))

        def load_groups(pool, tiles, rows, g, groups, name):
            tiles[g // groups] = pool.tile(
                [P, TILES_PER_GROUP * groups, rows.shape[3]], BF16, name=name, align_bytes=DMA_ALIGN
            )
            nc.sync.dma_start(out=tiles[g // groups][:], in_=in_dram(rows, TILES_PER_GROUP * g, TILES_PER_GROUP * groups))

        def group_of(tiles, g, groups):
            return tiles[g // groups][:, atoms_of(g % groups, 1), :]

        ident = consts.tile([P, P], F32, name="ident")
        make_identity(nc, ident[:])

        w_scales = consts.tile([P, N_BLOCKS * F], U8, name="w_scales", align_bytes=64)
        nc.vector.memset(w_scales[:].bitcast(I32), 0)
        bias_rows = consts.tile([P, F], BF16, name="bias_rows")
        nc.vector.memset(bias_rows[:], 0.0)
        nc.gpsimd.dma_start(
            out=bias_rows[0:N_BLOCKS, :], in_=b2.rearrange("(b f) -> b f", f=F)
        )

        load_h(0)
        w_words = consts.tile([P, 2 * N_BLOCKS * F], U8, name="w_words", align_bytes=64)
        nc.sync.dma_start(out=w_words[:].bitcast(I32), in_=W2_words[0].bitcast(I32))
        for quad in range(4):
            nc.sync.dma_start(
                out=w_scales[32 * quad : 32 * quad + 4, :].bitcast(I32),
                in_=W2_scales[0, 4 * quad : 4 * quad + 4, :].bitcast(I32),
            )
        for g in range(1, H_AHEAD + 1):
            load_h(g)
        for g in range(N_GROUPS):
            if g + H_AHEAD + 1 < N_GROUPS:
                load_h(g + H_AHEAD + 1)
            if g % Q_GROUPS == 0:
                load_groups(q_loads, mu_vw_sb, mu_vw_rows, g, Q_GROUPS, "mu_vw_sb")
            if g % MU_GROUPS == 0:
                load_groups(mu_loads, mu_w_sb, mu_w_rows, g, MU_GROUPS, "mu_w_sb")
            if g % Q_GROUPS == 0:
                load_groups(q_loads, q_sb, q_rows, g, Q_GROUPS, "q_sb")
            if g % MU_GROUPS == 0:
                load_groups(mu_loads, mu_sb, mu_rows, g, MU_GROUPS, "mu_sb")

        ident_bf16 = consts.tile([P, P], BF16, name="ident_bf16")
        nc.vector.tensor_copy(out=ident_bf16[:], in_=ident[:])
        bias_rows_f32 = consts.tile([P, F], F32, name="bias_rows_f32")
        bias_col = consts.tile([P, N_BLOCKS], F32, name="bias_col")

        def bias_to_partitions():
            nc.vector.tensor_copy(out=bias_rows_f32[:], in_=bias_rows[:])
            bias_bank = psum_b.tile([P, TILES_PER_GROUP, F], F32, name="x_bank")
            nc.tensor.transpose(out=bias_bank[:, 0, :], in_=bias_rows_f32[:], identity=ident[:])
            nc.scalar.activation(out=bias_col[:], in_=bias_bank[:, 0, 0:N_BLOCKS], func=IDENTITY)

        def transpose_h(g):
            words = h_sb[g][:].rearrange("p j k -> p (j k)").bitcast(F32)
            grouped_of[g] = regroup.tile(
                [P, TILES_PER_GROUP, P, PACK], BF16, name="grouped", align_bytes=64
            )
            grouped_words = (
                grouped_of[g][:]
                .rearrange("p j a t -> p (j a t)")
                .bitcast(F32)
                .rearrange("p (j a u) -> p j a u", j=TILES_PER_GROUP, u=2)
            )
            for first in range(0, TILES_PER_GROUP, TILES_PER_BANK):
                h_t = psum_h.tile([P, TILES_PER_BANK, 2, P], F32, name="h_t")
                for local in range(TILES_PER_BANK):
                    start = WORDS * (first + local)
                    for u in range(2):
                        nc.tensor.transpose(
                            out=h_t[:, local, u, :],
                            in_=words[:, start + u : start + WORDS : 2],
                            identity=ident[:],
                        )
                nc.scalar.copy(
                    out=grouped_words[:, first : first + TILES_PER_BANK, :, :],
                    in_=h_t[:].rearrange("p j u a -> p j a u"),
                )

        def quantise(g):
            codes_of[g] = stage.tile([P, GROUP_ATOMS], U32, name="codes", align_bytes=64)
            scales_of[g] = stage.tile([P, GROUP_ATOMS], U8, name="scales", align_bytes=64)
            nc.vector.quantize_mx(
                out=codes_of[g][:].bitcast(FP8X4),
                scales=scales_of[g][:],
                in_=grouped_of[g][:].rearrange("p j a t -> p (j a t)"),
            )

        def multiply(g):
            x_t_of[g] = {}
            for b in BLOCK_ORDER:
                acc = psum_x.tile([P, GROUP_ATOMS], F32, name="acc")
                nc.tensor.matmul_mx(
                    out=acc[:],
                    lhsT=w_words[:, 2 * F * b : 2 * F * (b + 1)].bitcast(FP4X4),
                    lhsT_scale=w_scales[:, F * b : F * (b + 1)],
                    rhs=codes_of[g][:].bitcast(FP8X4),
                    rhs_scale=scales_of[g][:],
                    start=True,
                    stop=True,
                )
                x_t_of[g][b] = biased.tile([P, GROUP_ATOMS], F32, name="x_t")
                nc.scalar.activation(
                    out=x_t_of[g][b][:],
                    in_=acc[:],
                    func=IDENTITY,
                    bias=bias_col[:, b : b + 1],
                    scale=1.0,
                )

        def turn_back(g):
            x_of[g] = {}
            for b in BLOCK_ORDER:
                x_of[g][b] = psum_b.tile([P, TILES_PER_GROUP, F], F32, name="x_bank")
                if b == DQ:
                    nc.tensor.matmul(
                        out=x_of[g][b][:].rearrange("p j f -> p (j f)"),
                        lhsT=ident_bf16[:],
                        rhs=group_of(q_sb, g, Q_GROUPS).rearrange("p j f -> p (j f)"),
                        start=True,
                        stop=False,
                    )
                for j in range(TILES_PER_GROUP):
                    nc.tensor.matmul(
                        out=x_of[g][b][:, j, :],
                        lhsT=x_t_of[g][b][:, P * j : P * (j + 1)],
                        rhs=ident[:],
                        is_transpose=True,
                        start=(b != DQ),
                        stop=(b != DQ or j == TILES_PER_GROUP - 1),
                    )

        def gate_q(g):
            q_gated_of[g] = stage.tile([P, TILES_PER_GROUP, F], F32, name="q_gated")
            nc.vector.tensor_tensor(
                out=q_gated_of[g][:],
                in0=x_of[g][DQMU][:],
                in1=group_of(mu_vw_sb, g, Q_GROUPS),
                op=MULT,
            )

        def sum_q(g):
            if g % Q_OUT_GROUPS == 0:
                q_new[g // Q_OUT_GROUPS] = q_outs.tile(
                    [P, TILES_PER_GROUP * Q_OUT_GROUPS, F], F32, name="q_new", align_bytes=DMA_ALIGN
                )
            nc.vector.tensor_tensor(
                out=group_of(q_new, g, Q_OUT_GROUPS),
                in0=x_of[g][DQ][:],
                in1=q_gated_of[g][:],
                op=ADD,
            )
            if g % Q_OUT_GROUPS == Q_OUT_GROUPS - 1:
                nc.sync.dma_start(
                    out=in_dram(q_out_rows, TILES_PER_GROUP * (g + 1 - Q_OUT_GROUPS), TILES_PER_GROUP * Q_OUT_GROUPS),
                    in_=q_new[g // Q_OUT_GROUPS][:],
                )

        def gate_mu(g):
            mu_new_of[g] = outs.tile(
                [P, TILES_PER_GROUP, C * F], F32, name="mu_new", align_bytes=DMA_ALIGN
            )
            nc.vector.tensor_tensor(
                out=mu_new_of[g][:].rearrange("p j (c f) -> p j c f", c=C),
                in0=x_of[g][DMU][:].unsqueeze(2).to_broadcast([P, TILES_PER_GROUP, C, F]),
                in1=group_of(mu_w_sb, g, MU_GROUPS).rearrange("p j (c f) -> p j c f", c=C),
                op=MULT,
            )

        def add_mu_and_store(engine, g, first, count):
            tiles = slice(first, first + count)
            engine.tensor_tensor(
                out=mu_new_of[g][:, tiles, :],
                in0=mu_new_of[g][:, tiles, :],
                in1=group_of(mu_sb, g, MU_GROUPS)[:, tiles, :],
                op=ADD,
            )
            nc.sync.dma_start(out=in_dram(mu_out_rows, TILES_PER_GROUP * g + first, count), in_=mu_new_of[g][:, tiles, :])

        def update_mu(g):
            if g < N_GROUPS - 1:
                add_mu_and_store(nc.gpsimd, g, 0, TILES_PER_GROUP)
            else:
                for first in range(0, TILES_PER_GROUP, TILES_PER_GROUP // 2):
                    add_mu_and_store(nc.vector, g, first, TILES_PER_GROUP // 2)

        transpose_h(0)
        bias_to_partitions()
        for s in range(N_GROUPS + 2):
            if s >= 2:
                turn_back(s - 2)
            if 1 <= s <= N_GROUPS:
                multiply(s - 1)
            if s + 1 < N_GROUPS:
                transpose_h(s + 1)
            if s >= 2:
                gate_q(s - 2)
                gate_mu(s - 2)
            if s < N_GROUPS:
                quantise(s)
            if s >= 2:
                sum_q(s - 2)
                update_mu(s - 2)
